import numpy as np
import ml_dtypes


def mxq(x, axis, fmt="e4m3"):
    dtype, down = {"e4m3": (ml_dtypes.float8_e4m3fn, 7), "e5m2": (ml_dtypes.float8_e5m2, 14)}[fmt]
    v = np.moveaxis(np.asarray(x, np.float32).astype(ml_dtypes.bfloat16).astype(np.float64), axis, -1)
    blocks = v.reshape(v.shape[:-1] + (-1, 32))
    amax = np.abs(blocks).max(-1, keepdims=True)
    byte = np.maximum(np.where(amax > 0, np.frexp(amax)[1] - 1 + 127, 0) - down, 1)
    scale = np.exp2(byte - 127.0)
    codes = (blocks / scale).astype(np.float32).astype(dtype).astype(np.float64)
    return np.moveaxis((codes * scale).reshape(v.shape), -1, axis)


WIDE = False


def mx_kscale(k):
    if not WIDE:
        return np.ones(k)
    levels = np.array([10, -10, 5, -5, 0])
    if k % 512:
        return np.exp2(np.random.permutation(np.resize(levels, k // 32))).repeat(32)
    a = np.empty((k // 512, 16))
    for p in range(k // 512):
        a[p, :8] = np.random.permutation(np.resize(levels, 8))
        for g in range(8):
            far = levels[np.abs(levels - a[p, g]) >= 10]
            a[p, g + 8] = far[np.random.randint(len(far))]
    return np.exp2(a.ravel()).repeat(32)


BF16 = ml_dtypes.bfloat16


def bf(x):
    return np.asarray(x, np.float32).astype(BF16)


def f64(x):
    return np.asarray(x).astype(np.float64)


B, S, HID, NH, HD, RD, RATIO = 1, 2048, 1024, 8, 128, 64, 4
THETA = 10000.0
NW = S // RATIO
HALF = RD // 2


def rope_tables(positions):
    inv_freq = 1.0 / THETA ** (np.arange(HALF) / HALF)
    ang = positions[:, None] * inv_freq[None, :]
    return np.cos(ang), np.sin(ang)


def rope_interleaved(x, cos, sin):
    nope, rope = x[..., :-RD], x[..., -RD:]
    pr = rope.reshape(rope.shape[:-1] + (HALF, 2))
    a, b = pr[..., 0], pr[..., 1]
    new = np.stack([a * cos - b * sin, a * sin + b * cos], axis=-1).reshape(rope.shape)
    return np.concatenate([nope, new], axis=-1)


def remap(t, fill):
    cur = t[..., HD:]
    prev = np.concatenate([np.full((B, 1, RATIO, HD), fill), t[:, :-1, :, :HD]], axis=1)
    return np.concatenate([prev, cur], axis=2)


def pool_overlap(kv, gate, ape):
    kv_o = remap(kv.reshape(B, NW, RATIO, 2 * HD), 0.0)
    gate_o = remap(gate.reshape(B, NW, RATIO, 2 * HD) + ape, -np.inf)
    e = np.exp(gate_o - gate_o.max(axis=2, keepdims=True))
    w = e / e.sum(axis=2, keepdims=True)
    return (kv_o * w).sum(axis=2)


def setup_inputs():
    s = mx_kscale(HID)
    return {"hidden": bf(np.random.standard_normal((B, S, HID)) * s),
            "wkv": bf(np.random.standard_normal((HID, 2 * HD)) * 2.0 / np.sqrt(HID) / s[:, None]),
            "wgate": bf(np.random.standard_normal((HID, 2 * HD)) / np.sqrt(HID) / s[:, None]),
            "ape": bf(np.random.standard_normal((RATIO, 2 * HD)) * 0.5)}


def reference(hidden, wkv, wgate, ape):
    hq = mxq(f64(hidden), 2, "e4m3")
    kv = hq @ mxq(f64(wkv), 0, "e4m3")
    gate = hq @ mxq(f64(wgate), 0, "e4m3")
    pooled = pool_overlap(kv, gate, f64(ape))
    ck, sk = rope_tables(np.arange(NW) * RATIO)
    k_rot = rope_interleaved(pooled, ck, sk)
    return k_rot, pooled

@@ -1,0 +1,292 @@
+import math
+from contextlib import ExitStack
+
+import concourse.mybir as mybir
+from concourse.masks import make_identity
+
+F32 = mybir.dt.float32
+BF16 = mybir.dt.bfloat16
+I32 = mybir.dt.int32
+U32 = mybir.dt.uint32
+U8 = mybir.dt.uint8
+FP8X4 = mybir.dt.float8_e4m3fn_x4
+ALU = mybir.AluOpType
+ACT = mybir.ActivationFunctionType
+
+P = 128
+S, HID, HD, RD, RATIO = 2048, 1024, 128, 64, 4
+THETA = 10000.0
+HALF = RD // 2
+NOPE = HD - RD
+PACK = 4
+PASSES = HID // (P * PACK)
+WINDOWS = S // RATIO
+TILES = WINDOWS // P
+SLOTS = 2 * RATIO
+LO, HI = 0, 1
+FINE = 8
+ROUND = 1.5 * 2.0**23
+
+FLOPS = 2 * S * HID * 4 * HD
+
+
+def tile_deepseekv4attention_pa_kernel(tc, hidden, wkv, wgate, ape, out_0, out_1):
+    nc = tc.nc
+    hidden_places = hidden.flatten_outer_dims().rearrange("(t i r) k -> r i t k", i=P, r=RATIO)
+    k_rot_rows = out_0.flatten_outer_dims().rearrange("(t i) f -> i t f", i=P)
+    pooled_rows = out_1.flatten_outer_dims().rearrange("(t i) f -> i t f", i=P)
+
+    with ExitStack() as ctx:
+        const = ctx.enter_context(tc.tile_pool(name="const", bufs=1))
+        weights = ctx.enter_context(tc.tile_pool(name="weights", bufs=2))
+        tokens = ctx.enter_context(tc.tile_pool(name="tokens", bufs=RATIO))
+        stage_in = ctx.enter_context(tc.tile_pool(name="stage_in", bufs=4))
+        soft = ctx.enter_context(tc.tile_pool(name="soft", bufs=1))
+        psum = ctx.enter_context(tc.psum_pool(name="psum", bufs=8))
+        ctx.enter_context(tc.manual_schedule())
+
+        def load_weight(w):
+            raw = weights.tile([P, PASSES, PACK, 2 * HD], BF16, name="w_raw")
+            nc.sync.dma_start(
+                out=raw[:].rearrange("p g t c -> p g (t c)"),
+                in_=w.rearrange("(g p t) c -> p g (t c)", p=P, t=PACK),
+            )
+            return raw
+
+        def load_place(r):
+            raw = tokens.tile([P, TILES, HID], BF16, name="x_raw")
+            for t in range(TILES):
+                nc.sync.dma_start(out=raw[:, t, :], in_=hidden_places[r][:, t, :])
+            return raw
+
+        ape_rows = const.tile([P, P], BF16)
+        nc.gpsimd.memset(ape_rows[:], 0.0)
+        nc.scalar.dma_start(out=ape_rows[0:SLOTS, :], in_=ape.rearrange("r (h f) -> (r h) f", h=2))
+        x_raw = [load_place(0)]
+        wgate_raw = load_weight(wgate)
+        x_raw.append(load_place(1))
+        wkv_raw = load_weight(wkv)
+        x_raw.extend([load_place(2), load_place(3)])
+
+        position_int = const.tile([P, TILES], I32)
+        nc.gpsimd.iota(position_int[:], pattern=[[RATIO * P, TILES]], base=0, channel_multiplier=RATIO)
+        position = const.tile([P, TILES], F32)
+        nc.vector.tensor_copy(out=position[:], in_=position_int[:])
+        ident = const.tile([P, P], F32)
+        make_identity(nc, ident[:])
+        turns = const.tile([P, TILES, HALF], F32)
+        for j in range(FINE):
+            nc.vector.tensor_single_scalar(
+                out=turns[:, :, j], in_=position[:], scalar=THETA ** (-j / HALF) / (2.0 * math.pi), op=ALU.mult
+            )
+        for j in range(FINE, HALF, FINE):
+            nc.vector.tensor_single_scalar(
+                out=turns[:, :, j : j + FINE], in_=turns[:, :, 0:FINE], scalar=THETA ** (-j / HALF), op=ALU.mult
+            )
+        whole_turns = const.tile([P, TILES, HALF], F32)
+        nc.vector.tensor_scalar(
+            out=whole_turns[:], in0=turns[:], scalar1=ROUND, scalar2=ROUND, op0=ALU.add, op1=ALU.subtract
+        )
+        phase = const.tile([P, 2, TILES, HALF], F32)
+        nc.vector.tensor_tensor(out=phase[:, 0], in0=turns[:], in1=whole_turns[:], op=ALU.subtract)
+        nc.vector.scalar_tensor_tensor(
+            out=phase[:, 1], in0=phase[:, 0], scalar=-1.0, in1=phase[:, 0], op0=ALU.mult, op1=ALU.min
+        )
+        nc.vector.tensor_single_scalar(out=phase[:, 1], in_=phase[:, 1], scalar=0.25, op=ALU.add)
+        sin_cos = const.tile([P, 2, TILES, HALF], F32)
+        nc.scalar.activation(out=sin_cos[:], in_=phase[:], func=ACT.Sin, scale=2.0 * math.pi)
+        neg_sin = const.tile([P, TILES, HALF], F32)
+        nc.scalar.activation(out=neg_sin[:], in_=phase[:, 0], func=ACT.Sin, scale=-2.0 * math.pi)
+
+        ape_col = const.tile([P, SLOTS], F32)
+
+        def spread_ape():
+            ape_rows_f32 = const.tile([P, P], F32)
+            nc.vector.tensor_copy(out=ape_rows_f32[:], in_=ape_rows[:])
+            ape_flip = psum.tile([P, PASSES * 2, P], F32, tag="bank")
+            nc.tensor.transpose(ape_flip[:, 0, :], ape_rows_f32[:], ident[:])
+            nc.vector.tensor_copy(out=ape_col[:], in_=ape_flip[:, 0, 0:SLOTS])
+
+        def offset(r, half):
+            return ape_col[:, 2 * r + half : 2 * r + half + 1]
+
+        weight = soft.tile([P, SLOTS, WINDOWS], F32)
+        weighted = soft.tile([P, SLOTS, WINDOWS], F32)
+        weight_pair = soft.tile([P, RATIO, WINDOWS], F32)
+        nc.vector.memset(weight[:, 0:RATIO, 0:1], 0.0)
+        nc.vector.memset(weighted[:, 0:RATIO, 0:1], 0.0)
+
+        def regroup_weight(raw, copy):
+            grouped = weights.tile([P, PASSES, 2 * HD, PACK], BF16, align_bytes=64, name="w_grouped")
+            for g in range(PASSES):
+                copy(
+                    out=grouped[:, g].rearrange("p (c i) t -> p c t i", i=4),
+                    in_=raw[:, g].rearrange("p t (c i) -> p c t i", i=4),
+                )
+            return grouped
+
+        def quantise_weight(grouped):
+            codes = weights.tile([P, PASSES, 2 * HD], U32, align_bytes=64, name="w_codes")
+            scales = weights.tile([P, PASSES, 2 * HD], U8, align_bytes=64, name="w_scales")
+            nc.vector.quantize_mx(
+                out=codes[:].rearrange("p g c -> p (g c)").bitcast(FP8X4),
+                scales=scales[:].rearrange("p g c -> p (g c)"),
+                in_=grouped[:].rearrange("p g c t -> p (g c t)"),
+            )
+            return codes, scales
+
+        def quantise_tiles(raw, pair, codes, scales):
+            words = raw[:].bitcast(F32)
+            grouped = stage_in.tile([P, PASSES, 2, P * PACK], BF16, align_bytes=64, name="x_grouped")
+            grouped_words = grouped[:].bitcast(F32)
+            for t2 in range(2):
+                flip = psum.tile([P, PASSES * 2, P], F32, tag="bank")
+                for g in range(PASSES):
+                    for u in range(2):
+                        nc.tensor.transpose(
+                            flip[:, 2 * g + u, :],
+                            words[:, 2 * pair + t2, 2 * P * g + u : 2 * P * (g + 1) : 2],
+                            ident[:],
+                        )
+                nc.scalar.copy(
+                    out=grouped_words[:, :, t2, :].rearrange("p g (i u) -> p g i u", u=2),
+                    in_=flip[:].rearrange("p (g u) i -> p g i u", u=2),
+                )
+            cols = slice(pair * 2 * P, (pair + 1) * 2 * P)
+            for g in range(PASSES):
+                nc.vector.quantize_mx(
+                    out=codes[:, g, cols].bitcast(FP8X4),
+                    scales=scales[:, g, cols],
+                    in_=grouped[:, g].rearrange("p t x -> p (t x)"),
+                )
+
+        def project(w, half, x):
+            w_codes, w_scales = w
+            x_codes, x_scales = x
+            features = slice(half * HD, (half + 1) * HD)
+            product = psum.tile([P, WINDOWS], F32, tag="bank")
+            for g in range(PASSES):
+                nc.tensor.matmul_mx(
+                    out=product[:],
+                    lhsT=w_codes[:, g, features].bitcast(FP8X4),
+                    lhsT_scale=w_scales[:, g, features],
+                    rhs=x_codes[:, g, :].bitcast(FP8X4),
+                    rhs_scale=x_scales[:, g, :],
+                    start=(g == 0),
+                    stop=(g == PASSES - 1),
+                )
+            return product
+
+        top = soft.tile([P, WINDOWS], F32)
+        x = []
+        gate = {}
+
+        def source(half):
+            return slice(0, WINDOWS - 1) if half == LO else slice(0, WINDOWS)
+
+        def window(half):
+            return slice(1, WINDOWS) if half == LO else slice(0, WINDOWS)
+
+        def gates_of_place(r):
+            for half in (HI, LO):
+                gate[(r, half)] = project(w_gate, half, x[r])
+                if r == 0 and half == HI:
+                    nc.vector.tensor_scalar(
+                        out=top[:], in0=gate[(r, half)][:], scalar1=offset(r, half), scalar2=None, op0=ALU.add
+                    )
+                else:
+                    nc.vector.scalar_tensor_tensor(
+                        out=top[:, window(half)], in0=gate[(r, half)][:, source(half)], scalar=offset(r, half),
+                        in1=top[:, window(half)], op0=ALU.add, op1=ALU.max,
+                    )
+
+        for r in range(RATIO + 1):
+            if r < RATIO:
+                codes = tokens.tile([P, PASSES, WINDOWS], U32, align_bytes=64, name="x_codes")
+                scales = tokens.tile([P, PASSES, WINDOWS], U8, align_bytes=64, name="x_scales")
+                x.append((codes, scales))
+                for pair in range(TILES // 2):
+                    quantise_tiles(x_raw[r], pair, codes, scales)
+            else:
+                table_warmer = const.tile([P, 1], F32)
+                nc.scalar.activation(out=table_warmer[:], in_=position[:, 0:1], func=ACT.Exp, scale=0.0)
+            if r == 0:
+                spread_ape()
+                w_gate = quantise_weight(regroup_weight(wgate_raw, nc.vector.tensor_copy))
+            else:
+                gates_of_place(r - 1)
+            if r == 1:
+                w_kv = quantise_weight(regroup_weight(wkv_raw, nc.vector.tensor_copy))
+
+        steps = [(r, half) for r in range(RATIO) for half in (LO, HI)]
+
+        for r, half in steps:
+            one = weight[:, half * RATIO + r, window(half)]
+            nc.vector.scalar_tensor_tensor(
+                out=one, in0=gate[(r, half)][:, source(half)], scalar=offset(r, half), in1=top[:, window(half)],
+                op0=ALU.add, op1=ALU.subtract,
+            )
+            nc.scalar.activation(out=one, in_=one, func=ACT.Exp)
+            if half == HI:
+                nc.gpsimd.tensor_tensor(
+                    out=weight_pair[:, r, :], in0=weight[:, r, :], in1=weight[:, RATIO + r, :], op=ALU.add
+                )
+
+        weight_sum = psum.tile([P, TILES, HD], F32, tag="bank")
+        weighted_sum = psum.tile([P, TILES, HD], F32, tag="bank")
+
+        def multiply_place(r):
+            for half in (LO, HI):
+                kv = project(w_kv, half, x[r])
+                slot = half * RATIO + r
+                nc.vector.tensor_tensor(
+                    out=weighted[:, slot, window(half)], in0=weight[:, slot, window(half)],
+                    in1=kv[:, source(half)], op=ALU.mult,
+                )
+
+        def add_up(total, terms, first, last):
+            for t in range(TILES):
+                nc.tensor.matmul(
+                    out=total[:, t, :], lhsT=terms[:, t * P : (t + 1) * P], rhs=ident[:], is_transpose=True,
+                    start=(first and t == 0), stop=(last and t == TILES - 1),
+                )
+
+        def add_weights(r):
+            add_up(weight_sum, weight_pair[:, r, :], r == 0, r == RATIO - 1)
+
+        def add_weighted(r):
+            for half in (LO, HI):
+                add_up(weighted_sum, weighted[:, half * RATIO + r, :], r == 0 and half == LO, r == RATIO - 1 and half == HI)
+
+        for r in range(RATIO - 1):
+            multiply_place(r)
+        add_weights(0)
+        add_weights(1)
+        add_weighted(0)
+        multiply_place(RATIO - 1)
+        add_weights(2)
+        add_weights(3)
+        for r in range(1, RATIO):
+            add_weighted(r)
+
+        root = soft.tile([P, TILES, HD], F32)
+        nc.scalar.activation(out=root[:], in_=weight_sum[:], func=ACT.Abs_reciprocal_sqrt)
+        inverse = soft.tile([P, TILES, HD], F32)
+        nc.scalar.activation(out=inverse[:], in_=root[:], func=ACT.Square)
+
+        pooled = soft.tile([P, TILES, HD], F32)
+        nc.vector.tensor_tensor(out=pooled[:], in0=weighted_sum[:], in1=inverse[:], op=ALU.mult)
+        nc.sync.dma_start(out=pooled_rows, in_=pooled[:])
+
+        k_rot = soft.tile([P, TILES, HD], F32)
+        nc.scalar.copy(out=k_rot[:, :, 0:NOPE], in_=pooled[:, :, 0:NOPE])
+        pairs = pooled[:, :, NOPE:HD].rearrange("p t (j e) -> p t j e", e=2)
+        turned = k_rot[:, :, NOPE:HD].rearrange("p t (j e) -> p t j e", e=2)
+        crossed = soft.tile([P, TILES, HALF, 2], F32)
+        nc.vector.tensor_tensor(
+            out=turned, in0=pairs, in1=sin_cos[:, 1].unsqueeze(3).to_broadcast([P, TILES, HALF, 2]), op=ALU.mult
+        )
+        nc.vector.tensor_tensor(out=crossed[:, :, :, 0], in0=pairs[:, :, :, 1], in1=neg_sin[:], op=ALU.mult)
+        nc.vector.tensor_tensor(out=crossed[:, :, :, 1], in0=pairs[:, :, :, 0], in1=sin_cos[:, 0], op=ALU.mult)
+        nc.vector.tensor_tensor(out=turned, in0=turned, in1=crossed[:], op=ALU.add)
+        nc.sync.dma_start(out=k_rot_rows, in_=k_rot[:])

@@ -62,9 +62,8 @@ def tile_deepseekv4attention_pa_kernel(tc, hidden, wkv, wgate, ape, out_0, out_1
         ape_rows = const.tile([P, P], BF16)
         nc.gpsimd.memset(ape_rows[:], 0.0)
         nc.scalar.dma_start(out=ape_rows[0:SLOTS, :], in_=ape.rearrange("r (h f) -> (r h) f", h=2))
-        x_raw = [load_place(0)]
         wgate_raw = load_weight(wgate)
-        x_raw.append(load_place(1))
+        x_raw = [load_place(0), load_place(1)]
         wkv_raw = load_weight(wkv)
         x_raw.extend([load_place(2), load_place(3)])
 
@@ -93,16 +92,17 @@ def tile_deepseekv4attention_pa_kernel(tc, hidden, wkv, wgate, ape, out_0, out_1
             out=phase[:, 1], in0=phase[:, 0], scalar=-1.0, in1=phase[:, 0], op0=ALU.mult, op1=ALU.min
         )
         nc.vector.tensor_single_scalar(out=phase[:, 1], in_=phase[:, 1], scalar=0.25, op=ALU.add)
-        sin_cos = const.tile([P, 2, TILES, HALF], F32)
-        nc.scalar.activation(out=sin_cos[:], in_=phase[:], func=ACT.Sin, scale=2.0 * math.pi)
-        neg_sin = const.tile([P, TILES, HALF], F32)
-        nc.scalar.activation(out=neg_sin[:], in_=phase[:, 0], func=ACT.Sin, scale=-2.0 * math.pi)
+        cos = const.tile([P, TILES, HALF], F32)
+        nc.scalar.activation(out=cos[:], in_=phase[:, 1], func=ACT.Sin, scale=2.0 * math.pi)
+        cross_sin = const.tile([P, TILES, HALF, 2], F32)
+        for e, sign in ((0, 1.0), (1, -1.0)):
+            nc.scalar.activation(out=cross_sin[:, :, :, e], in_=phase[:, 0], func=ACT.Sin, scale=sign * 2.0 * math.pi)
 
         ape_col = const.tile([P, SLOTS], F32)
+        ape_rows_f32 = const.tile([P, P], F32)
+        nc.scalar.copy(out=ape_rows_f32[:], in_=ape_rows[:])
 
         def spread_ape():
-            ape_rows_f32 = const.tile([P, P], F32)
-            nc.vector.tensor_copy(out=ape_rows_f32[:], in_=ape_rows[:])
             ape_flip = psum.tile([P, PASSES * 2, P], F32, tag="bank")
             nc.tensor.transpose(ape_flip[:, 0, :], ape_rows_f32[:], ident[:])
             nc.vector.tensor_copy(out=ape_col[:], in_=ape_flip[:, 0, 0:SLOTS])
@@ -112,7 +112,6 @@ def tile_deepseekv4attention_pa_kernel(tc, hidden, wkv, wgate, ape, out_0, out_1
 
         weight = soft.tile([P, SLOTS, WINDOWS], F32)
         weighted = soft.tile([P, SLOTS, WINDOWS], F32)
-        weight_pair = soft.tile([P, RATIO, WINDOWS], F32)
         nc.vector.memset(weight[:, 0:RATIO, 0:1], 0.0)
         nc.vector.memset(weighted[:, 0:RATIO, 0:1], 0.0)
 
@@ -135,30 +134,30 @@ def tile_deepseekv4attention_pa_kernel(tc, hidden, wkv, wgate, ape, out_0, out_1
             )
             return codes, scales
 
-        def quantise_tiles(raw, pair, codes, scales):
+        def transpose_place(raw):
             words = raw[:].bitcast(F32)
-            grouped = stage_in.tile([P, PASSES, 2, P * PACK], BF16, align_bytes=64, name="x_grouped")
+            grouped = stage_in.tile([P, PASSES, TILES, P * PACK], BF16, align_bytes=64, name="x_grouped")
             grouped_words = grouped[:].bitcast(F32)
-            for t2 in range(2):
+            for t in range(TILES):
                 flip = psum.tile([P, PASSES * 2, P], F32, tag="bank")
                 for g in range(PASSES):
                     for u in range(2):
                         nc.tensor.transpose(
-                            flip[:, 2 * g + u, :],
-                            words[:, 2 * pair + t2, 2 * P * g + u : 2 * P * (g + 1) : 2],
-                            ident[:],
+                            flip[:, 2 * g + u, :], words[:, t, 2 * P * g + u : 2 * P * (g + 1) : 2], ident[:]
                         )
                 nc.scalar.copy(
-                    out=grouped_words[:, :, t2, :].rearrange("p g (i u) -> p g i u", u=2),
+                    out=grouped_words[:, :, t, :].rearrange("p g (i u) -> p g i u", u=2),
                     in_=flip[:].rearrange("p (g u) i -> p g i u", u=2),
                 )
-            cols = slice(pair * 2 * P, (pair + 1) * 2 * P)
-            for g in range(PASSES):
-                nc.vector.quantize_mx(
-                    out=codes[:, g, cols].bitcast(FP8X4),
-                    scales=scales[:, g, cols],
-                    in_=grouped[:, g].rearrange("p t x -> p (t x)"),
-                )
+            return grouped
+
+        def quantise_tokens(grouped, g, first, last, x):
+            codes, scales = x
+            nc.vector.quantize_mx(
+                out=codes[:, g, first * P : last * P].bitcast(FP8X4),
+                scales=scales[:, g, first * P : last * P],
+                in_=grouped[:, g, first:last, :].rearrange("p t x -> p (t x)"),
+            )
 
         def project(w, half, x):
             w_codes, w_scales = w
@@ -177,6 +176,8 @@ def tile_deepseekv4attention_pa_kernel(tc, hidden, wkv, wgate, ape, out_0, out_1
                 )
             return product
 
+        first_gate = soft.tile([P, 2, WINDOWS], F32)
+        top_lo = soft.tile([P, WINDOWS], F32)
         top = soft.tile([P, WINDOWS], F32)
         x = []
         gate = {}
@@ -187,62 +188,107 @@ def tile_deepseekv4attention_pa_kernel(tc, hidden, wkv, wgate, ape, out_0, out_1
         def window(half):
             return slice(1, WINDOWS) if half == LO else slice(0, WINDOWS)
 
-        def gates_of_place(r):
+        def multiply_gates(r):
             for half in (HI, LO):
                 gate[(r, half)] = project(w_gate, half, x[r])
-                if r == 0 and half == HI:
-                    nc.vector.tensor_scalar(
-                        out=top[:], in0=gate[(r, half)][:], scalar1=offset(r, half), scalar2=None, op0=ALU.add
-                    )
-                else:
-                    nc.vector.scalar_tensor_tensor(
-                        out=top[:, window(half)], in0=gate[(r, half)][:, source(half)], scalar=offset(r, half),
-                        in1=top[:, window(half)], op0=ALU.add, op1=ALU.max,
-                    )
 
-        for r in range(RATIO + 1):
-            if r < RATIO:
-                codes = tokens.tile([P, PASSES, WINDOWS], U32, align_bytes=64, name="x_codes")
-                scales = tokens.tile([P, PASSES, WINDOWS], U8, align_bytes=64, name="x_scales")
-                x.append((codes, scales))
-                for pair in range(TILES // 2):
-                    quantise_tiles(x_raw[r], pair, codes, scales)
-            else:
-                table_warmer = const.tile([P, 1], F32)
-                nc.scalar.activation(out=table_warmer[:], in_=position[:, 0:1], func=ACT.Exp, scale=0.0)
-            if r == 0:
-                spread_ape()
-                w_gate = quantise_weight(regroup_weight(wgate_raw, nc.vector.tensor_copy))
-            else:
-                gates_of_place(r - 1)
-            if r == 1:
-                w_kv = quantise_weight(regroup_weight(wkv_raw, nc.vector.tensor_copy))
+        def split(half):
+            first = window(half).start
+            return [slice(first, WINDOWS // 2), slice(WINDOWS // 2, WINDOWS)]
 
-        steps = [(r, half) for r in range(RATIO) for half in (LO, HI)]
+        def shifted(half, part):
+            return slice(part.start - 1, part.stop - 1) if half == LO else part
 
-        for r, half in steps:
-            one = weight[:, half * RATIO + r, window(half)]
+        def raise_top(r, half, out, before, cols):
             nc.vector.scalar_tensor_tensor(
-                out=one, in0=gate[(r, half)][:, source(half)], scalar=offset(r, half), in1=top[:, window(half)],
-                op0=ALU.add, op1=ALU.subtract,
+                out=out, in0=gate[(r, half)][:, cols], scalar=offset(r, half), in1=before,
+                op0=ALU.add, op1=ALU.max,
             )
-            nc.scalar.activation(out=one, in_=one, func=ACT.Exp)
-            if half == HI:
-                nc.gpsimd.tensor_tensor(
-                    out=weight_pair[:, r, :], in0=weight[:, r, :], in1=weight[:, RATIO + r, :], op=ALU.add
-                )
 
-        weight_sum = psum.tile([P, TILES, HD], F32, tag="bank")
-        weighted_sum = psum.tile([P, TILES, HD], F32, tag="bank")
+        def largest_of_place(r):
+            if r == 0:
+                for half in (HI, LO):
+                    nc.scalar.activation(
+                        out=first_gate[:, half, :], in_=gate[(r, half)][:], func=ACT.Identity, bias=offset(r, half)
+                    )
+            elif r < RATIO - 1:
+                running = {HI: top, LO: top_lo}
+                for half in (HI, LO):
+                    cols = source(half)
+                    before = first_gate[:, half, cols] if r == 1 else running[half][:, cols]
+                    raise_top(r, half, running[half][:, cols], before, cols)
+            else:
+                for half in (HI, LO):
+                    for part in split(half):
+                        raise_top(r, half, top[:, part], top[:, part], shifted(half, part))
 
-        def multiply_place(r):
-            for half in (LO, HI):
-                kv = project(w_kv, half, x[r])
-                slot = half * RATIO + r
+        def join_tops():
+            for part in split(LO):
                 nc.vector.tensor_tensor(
-                    out=weighted[:, slot, window(half)], in0=weight[:, slot, window(half)],
-                    in1=kv[:, source(half)], op=ALU.mult,
+                    out=top[:, part], in0=top[:, part], in1=top_lo[:, shifted(LO, part)], op=ALU.max
                 )
+
+        wgate_grouped = regroup_weight(wgate_raw, nc.vector.tensor_copy)
+        w_gate = quantise_weight(wgate_grouped)
+
+        def take_in_place(r):
+            codes = tokens.tile([P, PASSES, WINDOWS], U32, align_bytes=64, name="x_codes")
+            scales = tokens.tile([P, PASSES, WINDOWS], U8, align_bytes=64, name="x_scales")
+            x.append((codes, scales))
+            grouped = transpose_place(x_raw[r])
+            for first in (0, TILES // 2):
+                for g in range(PASSES):
+                    quantise_tokens(grouped, g, first, first + TILES // 2, x[r])
+
+        take_in_place(0)
+        spread_ape()
+        take_in_place(1)
+        multiply_gates(0)
+        largest_of_place(0)
+        w_kv = quantise_weight(regroup_weight(wkv_raw, nc.vector.tensor_copy))
+        take_in_place(2)
+        multiply_gates(1)
+        largest_of_place(1)
+        take_in_place(3)
+        multiply_gates(2)
+        largest_of_place(2)
+        multiply_gates(3)
+        join_tops()
+        table_warmer = const.tile([P, 1], F32)
+        nc.scalar.activation(out=table_warmer[:], in_=position[:, 0:1], func=ACT.Exp, scale=0.0)
+
+        def lower(r, half, part=None):
+            part = part or window(half)
+            out = weight[:, half * RATIO + r, part]
+            cols = shifted(half, part)
+            if r == 0:
+                nc.gpsimd.tensor_tensor(out=out, in0=first_gate[:, half, cols], in1=top[:, part], op=ALU.subtract)
+            else:
+                nc.vector.scalar_tensor_tensor(
+                    out=out, in0=gate[(r, half)][:, cols], scalar=offset(r, half), in1=top[:, part],
+                    op0=ALU.add, op1=ALU.subtract,
+                )
+
+        def exponential(r, half):
+            one = weight[:, half * RATIO + r, window(half)]
+            nc.scalar.activation(out=one, in_=one, func=ACT.Exp)
+
+        kv = {}
+        kv_copy = soft.tile([P, 2, WINDOWS], F32)
+
+        def multiply_kv(r):
+            for half in (LO, HI):
+                kv[(r, half)] = project(w_kv, half, x[r])
+
+        def weigh(r, halves=(LO, HI)):
+            for half in halves:
+                slot = half * RATIO + r
+                out = weighted[:, slot, window(half)]
+                one = weight[:, slot, window(half)]
+                if r == 0:
+                    nc.gpsimd.tensor_tensor(out=out, in0=one, in1=kv_copy[:, half, source(half)], op=ALU.mult)
+                else:
+                    nc.vector.tensor_tensor(out=out, in0=one, in1=kv[(r, half)][:, source(half)], op=ALU.mult)
 
         def add_up(total, terms, first, last):
             for t in range(TILES):
@@ -251,42 +297,73 @@ def tile_deepseekv4attention_pa_kernel(tc, hidden, wkv, wgate, ape, out_0, out_1
                     start=(first and t == 0), stop=(last and t == TILES - 1),
                 )
 
-        def add_weights(r):
-            add_up(weight_sum, weight_pair[:, r, :], r == 0, r == RATIO - 1)
+        def add_all(total, terms, order, first=False, last=False):
+            for n, (r, half) in enumerate(order):
+                add_up(total, terms[:, half * RATIO + r, :], first and n == 0, last and n == len(order) - 1)
 
-        def add_weighted(r):
-            for half in (LO, HI):
-                add_up(weighted_sum, weighted[:, half * RATIO + r, :], r == 0 and half == LO, r == RATIO - 1 and half == HI)
-
-        for r in range(RATIO - 1):
-            multiply_place(r)
-        add_weights(0)
-        add_weights(1)
-        add_weighted(0)
-        multiply_place(RATIO - 1)
-        add_weights(2)
-        add_weights(3)
-        for r in range(1, RATIO):
-            add_weighted(r)
+        multiply_kv(0)
+        for half in (LO, HI):
+            nc.scalar.copy(out=kv_copy[:, half, :], in_=kv[(0, half)][:])
+        largest_of_place(RATIO - 1)
+        for half in (HI, LO):
+            lower(0, half)
+        for part in split(LO):
+            lower(1, LO, part)
+        lower(1, HI)
+        exponential(1, LO)
+        exponential(1, HI)
+        multiply_kv(1)
+        lower(2, LO)
+        lower(2, HI)
+        exponential(0, HI)
+        exponential(2, LO)
+        exponential(2, HI)
+        exponential(0, LO)
+        weigh(0, (HI,))
+        multiply_kv(2)
+        lower(3, LO)
+        lower(3, HI)
+        exponential(3, LO)
+        exponential(3, HI)
+        nc.scalar.activation(
+            out=table_warmer[:], in_=position[:, 0:1], func=ACT.Abs_reciprocal_sqrt, scale=0.0, bias=1.0
+        )
+        weigh(0, (LO,))
+        multiply_kv(3)
+        weight_sum = psum.tile([P, TILES, HD], F32, tag="bank")
+        weighted_sum = psum.tile([P, TILES, HD], F32, tag="bank")
+        for r in (1, 2, 3):
+            weigh(r)
+        add_all(weight_sum, weight, [(1, LO), (1, HI), (0, HI), (2, LO), (2, HI), (0, LO), (3, LO)], first=True)
+        add_all(weighted_sum, weighted, [(1, LO)], first=True)
+        add_all(weight_sum, weight, [(3, HI)], last=True)
+        add_all(
+            weighted_sum, weighted, [(1, HI), (0, HI), (2, LO), (2, HI), (0, LO), (3, LO), (3, HI)], last=True
+        )
 
         root = soft.tile([P, TILES, HD], F32)
         nc.scalar.activation(out=root[:], in_=weight_sum[:], func=ACT.Abs_reciprocal_sqrt)
         inverse = soft.tile([P, TILES, HD], F32)
         nc.scalar.activation(out=inverse[:], in_=root[:], func=ACT.Square)
 
+        shape = [P, TILES, HALF, 2]
+        in_pairs = "p t (j e) -> p t j e"
+        inverse_pairs = inverse[:, :, NOPE:HD].rearrange(in_pairs, e=2)
+        sum_pairs = weighted_sum[:, :, NOPE:HD].rearrange(in_pairs, e=2)
+        cos_inverse = soft.tile(shape, F32)
+        nc.vector.tensor_tensor(
+            out=cos_inverse[:], in0=inverse_pairs, in1=cos[:].unsqueeze(3).to_broadcast(shape), op=ALU.mult
+        )
+        sin_inverse = soft.tile(shape, F32)
+        nc.vector.tensor_tensor(out=sin_inverse[:], in0=inverse_pairs, in1=cross_sin[:], op=ALU.mult)
+        straight = soft.tile(shape, F32)
+        nc.vector.tensor_tensor(out=straight[:], in0=sum_pairs, in1=cos_inverse[:], op=ALU.mult)
+        crossed = soft.tile(shape, F32)
+        nc.vector.tensor_tensor(out=crossed[:], in0=sum_pairs, in1=sin_inverse[:], op=ALU.mult)
         pooled = soft.tile([P, TILES, HD], F32)
         nc.vector.tensor_tensor(out=pooled[:], in0=weighted_sum[:], in1=inverse[:], op=ALU.mult)
         nc.sync.dma_start(out=pooled_rows, in_=pooled[:])
-
-        k_rot = soft.tile([P, TILES, HD], F32)
-        nc.scalar.copy(out=k_rot[:, :, 0:NOPE], in_=pooled[:, :, 0:NOPE])
-        pairs = pooled[:, :, NOPE:HD].rearrange("p t (j e) -> p t j e", e=2)
-        turned = k_rot[:, :, NOPE:HD].rearrange("p t (j e) -> p t j e", e=2)
-        crossed = soft.tile([P, TILES, HALF, 2], F32)
-        nc.vector.tensor_tensor(
-            out=turned, in0=pairs, in1=sin_cos[:, 1].unsqueeze(3).to_broadcast([P, TILES, HALF, 2]), op=ALU.mult
-        )
-        nc.vector.tensor_tensor(out=crossed[:, :, :, 0], in0=pairs[:, :, :, 1], in1=neg_sin[:], op=ALU.mult)
-        nc.vector.tensor_tensor(out=crossed[:, :, :, 1], in0=pairs[:, :, :, 0], in1=sin_cos[:, 0], op=ALU.mult)
-        nc.vector.tensor_tensor(out=turned, in0=turned, in1=crossed[:], op=ALU.add)
-        nc.sync.dma_start(out=k_rot_rows, in_=k_rot[:])
+        nc.scalar.dma_start(out=k_rot_rows[:, :, 0:NOPE], in_=pooled[:, :, 0:NOPE])
+        turned = soft.tile(shape, F32)
+        nc.vector.tensor_tensor(out=turned[:], in0=straight[:], in1=crossed[:, :, :, ::-1], op=ALU.add)
+        nc.sync.dma_start(out=k_rot_rows[:, :, NOPE:HD], in_=turned[:].rearrange("p t j e -> p t (j e)"))

@@ -53,19 +53,21 @@ def tile_deepseekv4attention_pa_kernel(tc, hidden, wkv, wgate, ape, out_0, out_1
             )
             return raw
 
-        def load_place(r):
-            raw = tokens.tile([P, TILES, HID], BF16, name="x_raw")
-            for t in range(TILES):
-                nc.sync.dma_start(out=raw[:, t, :], in_=hidden_places[r][:, t, :])
-            return raw
+        def load_tiles(r, tiles):
+            for t in tiles:
+                nc.sync.dma_start(out=x_raw[r][:, t, :], in_=hidden_places[r][:, t, :])
 
         ape_rows = const.tile([P, P], BF16)
         nc.gpsimd.memset(ape_rows[:], 0.0)
         nc.scalar.dma_start(out=ape_rows[0:SLOTS, :], in_=ape.rearrange("r (h f) -> (r h) f", h=2))
+        x_raw = [tokens.tile([P, TILES, HID], BF16, name="x_raw") for r in range(RATIO)]
+        load_tiles(0, range(0, TILES // 2))
         wgate_raw = load_weight(wgate)
-        x_raw = [load_place(0), load_place(1)]
+        load_tiles(0, range(TILES // 2, TILES))
+        load_tiles(1, range(TILES))
         wkv_raw = load_weight(wkv)
-        x_raw.extend([load_place(2), load_place(3)])
+        load_tiles(2, range(TILES))
+        load_tiles(3, range(TILES))
 
         position_int = const.tile([P, TILES], I32)
         nc.gpsimd.iota(position_int[:], pattern=[[RATIO * P, TILES]], base=0, channel_multiplier=RATIO)
@@ -211,12 +213,11 @@ def tile_deepseekv4attention_pa_kernel(tc, hidden, wkv, wgate, ape, out_0, out_1
                     nc.scalar.activation(
                         out=first_gate[:, half, :], in_=gate[(r, half)][:], func=ACT.Identity, bias=offset(r, half)
                     )
-            elif r < RATIO - 1:
-                running = {HI: top, LO: top_lo}
-                for half in (HI, LO):
+            elif r == 1:
+                for half, running in ((HI, top), (LO, top_lo)):
                     cols = source(half)
-                    before = first_gate[:, half, cols] if r == 1 else running[half][:, cols]
-                    raise_top(r, half, running[half][:, cols], before, cols)
+                    raise_top(r, half, running[:, cols], first_gate[:, half, cols], cols)
+                join_tops()
             else:
                 for half in (HI, LO):
                     for part in split(half):
@@ -253,7 +254,6 @@ def tile_deepseekv4attention_pa_kernel(tc, hidden, wkv, wgate, ape, out_0, out_1
         multiply_gates(2)
         largest_of_place(2)
         multiply_gates(3)
-        join_tops()
         table_warmer = const.tile([P, 1], F32)
         nc.scalar.activation(out=table_warmer[:], in_=position[:, 0:1], func=ACT.Exp, scale=0.0)
 

@@ -363,7 +363,9 @@ def tile_deepseekv4attention_pa_kernel(tc, hidden, wkv, wgate, ape, out_0, out_1
         pooled = soft.tile([P, TILES, HD], F32)
         nc.vector.tensor_tensor(out=pooled[:], in0=weighted_sum[:], in1=inverse[:], op=ALU.mult)
         nc.sync.dma_start(out=pooled_rows, in_=pooled[:])
-        nc.scalar.dma_start(out=k_rot_rows[:, :, 0:NOPE], in_=pooled[:, :, 0:NOPE])
-        turned = soft.tile(shape, F32)
-        nc.vector.tensor_tensor(out=turned[:], in0=straight[:], in1=crossed[:, :, :, ::-1], op=ALU.add)
-        nc.sync.dma_start(out=k_rot_rows[:, :, NOPE:HD], in_=turned[:].rearrange("p t j e -> p t (j e)"))
+        k_rot = soft.tile([P, TILES, HD], F32)
+        nc.scalar.copy(out=k_rot[:, :, 0:NOPE], in_=pooled[:, :, 0:NOPE])
+        nc.vector.tensor_tensor(
+            out=k_rot[:, :, NOPE:HD].rearrange(in_pairs, e=2), in0=straight[:], in1=crossed[:, :, :, ::-1], op=ALU.add
+        )
+        nc.sync.dma_start(out=k_rot_rows, in_=k_rot[:])

@@ -53,21 +53,21 @@ def tile_deepseekv4attention_pa_kernel(tc, hidden, wkv, wgate, ape, out_0, out_1
             )
             return raw
 
-        def load_tiles(r, tiles):
-            for t in tiles:
-                nc.sync.dma_start(out=x_raw[r][:, t, :], in_=hidden_places[r][:, t, :])
+        def load_tiles(r, *parts):
+            for first, last in parts:
+                nc.sync.dma_start(out=x_raw[r][:, first:last, :], in_=hidden_places[r][:, first:last, :])
 
         ape_rows = const.tile([P, P], BF16)
         nc.gpsimd.memset(ape_rows[:], 0.0)
         nc.scalar.dma_start(out=ape_rows[0:SLOTS, :], in_=ape.rearrange("r (h f) -> (r h) f", h=2))
         x_raw = [tokens.tile([P, TILES, HID], BF16, name="x_raw") for r in range(RATIO)]
-        load_tiles(0, range(0, TILES // 2))
+        load_tiles(0, (0, 1), (1, 2))
         wgate_raw = load_weight(wgate)
-        load_tiles(0, range(TILES // 2, TILES))
-        load_tiles(1, range(TILES))
+        load_tiles(0, (2, 4))
+        load_tiles(1, (0, 2), (2, 4))
         wkv_raw = load_weight(wkv)
-        load_tiles(2, range(TILES))
-        load_tiles(3, range(TILES))
+        load_tiles(2, (0, 2), (2, 4))
+        load_tiles(3, (0, 2), (2, 3), (3, 4))
 
         position_int = const.tile([P, TILES], I32)
         nc.gpsimd.iota(position_int[:], pattern=[[RATIO * P, TILES]], base=0, channel_multiplier=RATIO)
@@ -269,8 +269,8 @@ def tile_deepseekv4attention_pa_kernel(tc, hidden, wkv, wgate, ape, out_0, out_1
                     op0=ALU.add, op1=ALU.subtract,
                 )
 
-        def exponential(r, half):
-            one = weight[:, half * RATIO + r, window(half)]
+        def exponential(r, half, part=None):
+            one = weight[:, half * RATIO + r, part or window(half)]
             nc.scalar.activation(out=one, in_=one, func=ACT.Exp)
 
         kv = {}
@@ -309,8 +309,8 @@ def tile_deepseekv4attention_pa_kernel(tc, hidden, wkv, wgate, ape, out_0, out_1
             lower(0, half)
         for part in split(LO):
             lower(1, LO, part)
+            exponential(1, LO, part)
         lower(1, HI)
-        exponential(1, LO)
         exponential(1, HI)
         multiply_kv(1)
         lower(2, LO)
@@ -342,9 +342,12 @@ def tile_deepseekv4attention_pa_kernel(tc, hidden, wkv, wgate, ape, out_0, out_1
         )
 
         root = soft.tile([P, TILES, HD], F32)
-        nc.scalar.activation(out=root[:], in_=weight_sum[:], func=ACT.Abs_reciprocal_sqrt)
         inverse = soft.tile([P, TILES, HD], F32)
-        nc.scalar.activation(out=inverse[:], in_=root[:], func=ACT.Square)
+        sides = [slice(0, TILES // 2), slice(TILES // 2, TILES)]
+        for side in sides:
+            nc.scalar.activation(out=root[:, side, :], in_=weight_sum[:, side, :], func=ACT.Abs_reciprocal_sqrt)
+        for side in sides:
+            nc.scalar.activation(out=inverse[:, side, :], in_=root[:, side, :], func=ACT.Square)
 
         shape = [P, TILES, HALF, 2]
         in_pairs = "p t (j e) -> p t j e"

@@ -136,46 +136,50 @@ def tile_deepseekv4attention_pa_kernel(tc, hidden, wkv, wgate, ape, out_0, out_1
             )
             return codes, scales
 
-        def transpose_place(raw):
+        def transpose_pair(raw, pair):
             words = raw[:].bitcast(F32)
-            grouped = stage_in.tile([P, PASSES, TILES, P * PACK], BF16, align_bytes=64, name="x_grouped")
+            grouped = stage_in.tile([P, PASSES, 2, P * PACK], BF16, align_bytes=64, name="x_grouped")
             grouped_words = grouped[:].bitcast(F32)
-            for t in range(TILES):
+            for t2 in range(2):
                 flip = psum.tile([P, PASSES * 2, P], F32, tag="bank")
                 for g in range(PASSES):
                     for u in range(2):
                         nc.tensor.transpose(
-                            flip[:, 2 * g + u, :], words[:, t, 2 * P * g + u : 2 * P * (g + 1) : 2], ident[:]
+                            flip[:, 2 * g + u, :], words[:, 2 * pair + t2, 2 * P * g + u : 2 * P * (g + 1) : 2], ident[:]
                         )
                 nc.scalar.copy(
-                    out=grouped_words[:, :, t, :].rearrange("p g (i u) -> p g i u", u=2),
+                    out=grouped_words[:, :, t2, :].rearrange("p g (i u) -> p g i u", u=2),
                     in_=flip[:].rearrange("p (g u) i -> p g i u", u=2),
                 )
             return grouped
 
-        def quantise_tokens(grouped, g, first, last, x):
+        def quantise_pair(grouped, x, pair):
             codes, scales = x
             nc.vector.quantize_mx(
-                out=codes[:, g, first * P : last * P].bitcast(FP8X4),
-                scales=scales[:, g, first * P : last * P],
-                in_=grouped[:, g, first:last, :].rearrange("p t x -> p (t x)"),
+                out=codes[:, pair].rearrange("p g c -> p (g c)").bitcast(FP8X4),
+                scales=scales[:, pair].rearrange("p g c -> p (g c)"),
+                in_=grouped[:].rearrange("p g t x -> p (g t x)"),
             )
 
-        def project(w, half, x):
+        def add_passes(product, w, half, x, pair):
             w_codes, w_scales = w
             x_codes, x_scales = x
             features = slice(half * HD, (half + 1) * HD)
-            product = psum.tile([P, WINDOWS], F32, tag="bank")
             for g in range(PASSES):
                 nc.tensor.matmul_mx(
-                    out=product[:],
+                    out=product[:, pair * 2 * P : (pair + 1) * 2 * P],
                     lhsT=w_codes[:, g, features].bitcast(FP8X4),
                     lhsT_scale=w_scales[:, g, features],
-                    rhs=x_codes[:, g, :].bitcast(FP8X4),
-                    rhs_scale=x_scales[:, g, :],
+                    rhs=x_codes[:, pair, g, :].bitcast(FP8X4),
+                    rhs_scale=x_scales[:, pair, g, :],
                     start=(g == 0),
                     stop=(g == PASSES - 1),
                 )
+
+        def project(w, half, x):
+            product = psum.tile([P, WINDOWS], F32, tag="bank")
+            for pair in range(TILES // 2):
+                add_passes(product, w, half, x, pair)
             return product
 
         first_gate = soft.tile([P, 2, WINDOWS], F32)
@@ -193,6 +197,14 @@ def tile_deepseekv4attention_pa_kernel(tc, hidden, wkv, wgate, ape, out_0, out_1
         def multiply_gates(r):
             for half in (HI, LO):
                 gate[(r, half)] = project(w_gate, half, x[r])
+
+        def multiply_last_gates():
+            r = RATIO - 1
+            for half in (HI, LO):
+                gate[(r, half)] = psum.tile([P, WINDOWS], F32, tag="bank", name="product")
+            for pair in range(TILES // 2):
+                for half in (HI, LO):
+                    add_passes(gate[(r, half)], w_gate, half, x[r], pair)
 
         def split(half):
             first = window(half).start
@@ -233,13 +245,11 @@ def tile_deepseekv4attention_pa_kernel(tc, hidden, wkv, wgate, ape, out_0, out_1
         w_gate = quantise_weight(wgate_grouped)
 
         def take_in_place(r):
-            codes = tokens.tile([P, PASSES, WINDOWS], U32, align_bytes=64, name="x_codes")
-            scales = tokens.tile([P, PASSES, WINDOWS], U8, align_bytes=64, name="x_scales")
+            codes = tokens.tile([P, TILES // 2, PASSES, 2 * P], U32, align_bytes=64, name="x_codes")
+            scales = tokens.tile([P, TILES // 2, PASSES, 2 * P], U8, align_bytes=64, name="x_scales")
             x.append((codes, scales))
-            grouped = transpose_place(x_raw[r])
-            for first in (0, TILES // 2):
-                for g in range(PASSES):
-                    quantise_tokens(grouped, g, first, first + TILES // 2, x[r])
+            for pair in range(TILES // 2):
+                quantise_pair(transpose_pair(x_raw[r], pair), x[r], pair)
 
         take_in_place(0)
         spread_ape()
@@ -253,7 +263,7 @@ def tile_deepseekv4attention_pa_kernel(tc, hidden, wkv, wgate, ape, out_0, out_1
         take_in_place(3)
         multiply_gates(2)
         largest_of_place(2)
-        multiply_gates(3)
+        multiply_last_gates()
         table_warmer = const.tile([P, 1], F32)
         nc.scalar.activation(out=table_warmer[:], in_=position[:, 0:1], func=ACT.Exp, scale=0.0)
 

@@ -61,9 +61,8 @@ def tile_deepseekv4attention_pa_kernel(tc, hidden, wkv, wgate, ape, out_0, out_1
         nc.gpsimd.memset(ape_rows[:], 0.0)
         nc.scalar.dma_start(out=ape_rows[0:SLOTS, :], in_=ape.rearrange("r (h f) -> (r h) f", h=2))
         x_raw = [tokens.tile([P, TILES, HID], BF16, name="x_raw") for r in range(RATIO)]
-        load_tiles(0, (0, 1), (1, 2))
         wgate_raw = load_weight(wgate)
-        load_tiles(0, (2, 4))
+        load_tiles(0, (0, 2), (2, 4))
         load_tiles(1, (0, 2), (2, 4))
         wkv_raw = load_weight(wkv)
         load_tiles(2, (0, 2), (2, 4))
@@ -102,7 +101,6 @@ def tile_deepseekv4attention_pa_kernel(tc, hidden, wkv, wgate, ape, out_0, out_1
 
         ape_col = const.tile([P, SLOTS], F32)
         ape_rows_f32 = const.tile([P, P], F32)
-        nc.scalar.copy(out=ape_rows_f32[:], in_=ape_rows[:])
 
         def spread_ape():
             ape_flip = psum.tile([P, PASSES * 2, P], F32, tag="bank")
@@ -114,6 +112,7 @@ def tile_deepseekv4attention_pa_kernel(tc, hidden, wkv, wgate, ape, out_0, out_1
 
         weight = soft.tile([P, SLOTS, WINDOWS], F32)
         weighted = soft.tile([P, SLOTS, WINDOWS], F32)
+        weighted_pair = soft.tile([P, 2, WINDOWS], F32)
         nc.vector.memset(weight[:, 0:RATIO, 0:1], 0.0)
         nc.vector.memset(weighted[:, 0:RATIO, 0:1], 0.0)
 
@@ -219,7 +218,7 @@ def tile_deepseekv4attention_pa_kernel(tc, hidden, wkv, wgate, ape, out_0, out_1
                 op0=ALU.add, op1=ALU.max,
             )
 
-        def largest_of_place(r):
+        def largest_of_place(r, halves=(HI, LO)):
             if r == 0:
                 for half in (HI, LO):
                     nc.scalar.activation(
@@ -229,9 +228,8 @@ def tile_deepseekv4attention_pa_kernel(tc, hidden, wkv, wgate, ape, out_0, out_1
                 for half, running in ((HI, top), (LO, top_lo)):
                     cols = source(half)
                     raise_top(r, half, running[:, cols], first_gate[:, half, cols], cols)
-                join_tops()
             else:
-                for half in (HI, LO):
+                for half in halves:
                     for part in split(half):
                         raise_top(r, half, top[:, part], top[:, part], shifted(half, part))
 
@@ -244,25 +242,39 @@ def tile_deepseekv4attention_pa_kernel(tc, hidden, wkv, wgate, ape, out_0, out_1
         wgate_grouped = regroup_weight(wgate_raw, nc.vector.tensor_copy)
         w_gate = quantise_weight(wgate_grouped)
 
-        def take_in_place(r):
-            codes = tokens.tile([P, TILES // 2, PASSES, 2 * P], U32, align_bytes=64, name="x_codes")
-            scales = tokens.tile([P, TILES // 2, PASSES, 2 * P], U8, align_bytes=64, name="x_scales")
-            x.append((codes, scales))
-            for pair in range(TILES // 2):
-                quantise_pair(transpose_pair(x_raw[r], pair), x[r], pair)
+        def take_in_pair(r, pair):
+            if pair == 0:
+                codes = tokens.tile([P, TILES // 2, PASSES, 2 * P], U32, align_bytes=64, name="x_codes")
+                scales = tokens.tile([P, TILES // 2, PASSES, 2 * P], U8, align_bytes=64, name="x_scales")
+                x.append((codes, scales))
+            return transpose_pair(x_raw[r], pair)
 
-        take_in_place(0)
+        nc.vector.tensor_copy(out=ape_rows_f32[:], in_=ape_rows[:])
+        for pair in range(TILES // 2):
+            quantise_pair(take_in_pair(0, pair), x[0], pair)
         spread_ape()
-        take_in_place(1)
+
+        quantise_pair(take_in_pair(1, 0), x[1], 0)
+        second = take_in_pair(1, 1)
+        wkv_grouped = regroup_weight(wkv_raw, nc.vector.tensor_copy)
+        quantise_pair(second, x[1], 1)
         multiply_gates(0)
         largest_of_place(0)
-        w_kv = quantise_weight(regroup_weight(wkv_raw, nc.vector.tensor_copy))
-        take_in_place(2)
+        w_kv = quantise_weight(wkv_grouped)
+
+        quantise_pair(take_in_pair(2, 0), x[2], 0)
+        second = take_in_pair(2, 1)
         multiply_gates(1)
         largest_of_place(1)
-        take_in_place(3)
+        quantise_pair(second, x[2], 1)
+        join_tops()
+
+        quantise_pair(take_in_pair(3, 0), x[3], 0)
+        second = take_in_pair(3, 1)
         multiply_gates(2)
-        largest_of_place(2)
+        largest_of_place(2, (HI,))
+        quantise_pair(second, x[3], 1)
+        largest_of_place(2, (LO,))
         multiply_last_gates()
         table_warmer = const.tile([P, 1], F32)
         nc.scalar.activation(out=table_warmer[:], in_=position[:, 0:1], func=ACT.Exp, scale=0.0)
@@ -344,12 +356,14 @@ def tile_deepseekv4attention_pa_kernel(tc, hidden, wkv, wgate, ape, out_0, out_1
         weighted_sum = psum.tile([P, TILES, HD], F32, tag="bank")
         for r in (1, 2, 3):
             weigh(r)
+        for slot, (r, add) in enumerate(((2, nc.gpsimd.tensor_tensor), (3, nc.vector.tensor_tensor))):
+            add(out=weighted_pair[:, slot, :], in0=weighted[:, r, :], in1=weighted[:, RATIO + r, :], op=ALU.add)
         add_all(weight_sum, weight, [(1, LO), (1, HI), (0, HI), (2, LO), (2, HI), (0, LO), (3, LO)], first=True)
         add_all(weighted_sum, weighted, [(1, LO)], first=True)
         add_all(weight_sum, weight, [(3, HI)], last=True)
-        add_all(
-            weighted_sum, weighted, [(1, HI), (0, HI), (2, LO), (2, HI), (0, LO), (3, LO), (3, HI)], last=True
-        )
+        add_all(weighted_sum, weighted, [(1, HI), (0, HI), (0, LO)])
+        for slot in (0, 1):
+            add_up(weighted_sum, weighted_pair[:, slot, :], False, slot == 1)
 
         root = soft.tile([P, TILES, HD], F32)
         inverse = soft.tile([P, TILES, HD], F32)

import math
from contextlib import ExitStack

import concourse.mybir as mybir
from concourse.masks import make_identity

F32 = mybir.dt.float32
BF16 = mybir.dt.bfloat16
I32 = mybir.dt.int32
U32 = mybir.dt.uint32
U8 = mybir.dt.uint8
FP8X4 = mybir.dt.float8_e4m3fn_x4
ALU = mybir.AluOpType
ACT = mybir.ActivationFunctionType

P = 128
S, HID, HD, RD, RATIO = 2048, 1024, 128, 64, 4
THETA = 10000.0
HALF = RD // 2
NOPE = HD - RD
PACK = 4
PASSES = HID // (P * PACK)
WINDOWS = S // RATIO
TILES = WINDOWS // P
SLOTS = 2 * RATIO
LO, HI = 0, 1
FINE = 8
ROUND = 1.5 * 2.0**23

FLOPS = 2 * S * HID * 4 * HD


def tile_deepseekv4attention_pa_kernel(tc, hidden, wkv, wgate, ape, out_0, out_1):
    nc = tc.nc
    hidden_places = hidden.flatten_outer_dims().rearrange("(t i r) k -> r i t k", i=P, r=RATIO)
    k_rot_rows = out_0.flatten_outer_dims().rearrange("(t i) f -> i t f", i=P)
    pooled_rows = out_1.flatten_outer_dims().rearrange("(t i) f -> i t f", i=P)

    with ExitStack() as ctx:
        const = ctx.enter_context(tc.tile_pool(name="const", bufs=1))
        weights = ctx.enter_context(tc.tile_pool(name="weights", bufs=2))
        tokens = ctx.enter_context(tc.tile_pool(name="tokens", bufs=RATIO))
        stage_in = ctx.enter_context(tc.tile_pool(name="stage_in", bufs=4))
        soft = ctx.enter_context(tc.tile_pool(name="soft", bufs=1))
        psum = ctx.enter_context(tc.psum_pool(name="psum", bufs=8))
        ctx.enter_context(tc.manual_schedule())

        def load_weight(w):
            raw = weights.tile([P, PASSES, PACK, 2 * HD], BF16, name="w_raw")
            nc.sync.dma_start(
                out=raw[:].rearrange("p g t c -> p g (t c)"),
                in_=w.rearrange("(g p t) c -> p g (t c)", p=P, t=PACK),
            )
            return raw

        def load_tiles(r, *parts):
            for first, last in parts:
                nc.sync.dma_start(out=x_raw[r][:, first:last, :], in_=hidden_places[r][:, first:last, :])

        ape_rows = const.tile([P, P], BF16)
        nc.gpsimd.memset(ape_rows[:], 0.0)
        nc.scalar.dma_start(out=ape_rows[0:SLOTS, :], in_=ape.rearrange("r (h f) -> (r h) f", h=2))
        x_raw = [tokens.tile([P, TILES, HID], BF16, name="x_raw") for r in range(RATIO)]
        wgate_raw = load_weight(wgate)
        load_tiles(0, (0, 2), (2, 4))
        load_tiles(1, (0, 2), (2, 4))
        wkv_raw = load_weight(wkv)
        load_tiles(2, (0, 2), (2, 4))
        load_tiles(3, (0, 2), (2, 3), (3, 4))

        position_int = const.tile([P, TILES], I32)
        nc.gpsimd.iota(position_int[:], pattern=[[RATIO * P, TILES]], base=0, channel_multiplier=RATIO)
        position = const.tile([P, TILES], F32)
        nc.vector.tensor_copy(out=position[:], in_=position_int[:])
        ident = const.tile([P, P], F32)
        make_identity(nc, ident[:])
        turns = const.tile([P, TILES, HALF], F32)
        for j in range(FINE):
            nc.vector.tensor_single_scalar(
                out=turns[:, :, j], in_=position[:], scalar=THETA ** (-j / HALF) / (2.0 * math.pi), op=ALU.mult
            )
        for j in range(FINE, HALF, FINE):
            nc.vector.tensor_single_scalar(
                out=turns[:, :, j : j + FINE], in_=turns[:, :, 0:FINE], scalar=THETA ** (-j / HALF), op=ALU.mult
            )
        whole_turns = const.tile([P, TILES, HALF], F32)
        nc.vector.tensor_scalar(
            out=whole_turns[:], in0=turns[:], scalar1=ROUND, scalar2=ROUND, op0=ALU.add, op1=ALU.subtract
        )
        phase = const.tile([P, 2, TILES, HALF], F32)
        nc.vector.tensor_tensor(out=phase[:, 0], in0=turns[:], in1=whole_turns[:], op=ALU.subtract)
        nc.vector.scalar_tensor_tensor(
            out=phase[:, 1], in0=phase[:, 0], scalar=-1.0, in1=phase[:, 0], op0=ALU.mult, op1=ALU.min
        )
        nc.vector.tensor_single_scalar(out=phase[:, 1], in_=phase[:, 1], scalar=0.25, op=ALU.add)
        cos = const.tile([P, TILES, HALF], F32)
        nc.scalar.activation(out=cos[:], in_=phase[:, 1], func=ACT.Sin, scale=2.0 * math.pi)
        cross_sin = const.tile([P, TILES, HALF, 2], F32)
        for e, sign in ((0, 1.0), (1, -1.0)):
            nc.scalar.activation(out=cross_sin[:, :, :, e], in_=phase[:, 0], func=ACT.Sin, scale=sign * 2.0 * math.pi)

        ape_col = const.tile([P, SLOTS], F32)
        ape_rows_f32 = const.tile([P, P], F32)

        def spread_ape():
            ape_flip = psum.tile([P, PASSES * 2, P], F32, tag="bank")
            nc.tensor.transpose(ape_flip[:, 0, :], ape_rows_f32[:], ident[:])
            nc.vector.tensor_copy(out=ape_col[:], in_=ape_flip[:, 0, 0:SLOTS])

        def offset(r, half):
            return ape_col[:, 2 * r + half : 2 * r + half + 1]

        weight = soft.tile([P, SLOTS, WINDOWS], F32)
        weighted = soft.tile([P, SLOTS, WINDOWS], F32)
        weighted_pair = soft.tile([P, 2, WINDOWS], F32)
        nc.vector.memset(weight[:, 0:RATIO, 0:1], 0.0)
        nc.vector.memset(weighted[:, 0:RATIO, 0:1], 0.0)

        def regroup_weight(raw, copy):
            grouped = weights.tile([P, PASSES, 2 * HD, PACK], BF16, align_bytes=64, name="w_grouped")
            for g in range(PASSES):
                copy(
                    out=grouped[:, g].rearrange("p (c i) t -> p c t i", i=4),
                    in_=raw[:, g].rearrange("p t (c i) -> p c t i", i=4),
                )
            return grouped

        def quantise_weight(grouped):
            codes = weights.tile([P, PASSES, 2 * HD], U32, align_bytes=64, name="w_codes")
            scales = weights.tile([P, PASSES, 2 * HD], U8, align_bytes=64, name="w_scales")
            nc.vector.quantize_mx(
                out=codes[:].rearrange("p g c -> p (g c)").bitcast(FP8X4),
                scales=scales[:].rearrange("p g c -> p (g c)"),
                in_=grouped[:].rearrange("p g c t -> p (g c t)"),
            )
            return codes, scales

        def transpose_pair(raw, pair):
            words = raw[:].bitcast(F32)
            grouped = stage_in.tile([P, PASSES, 2, P * PACK], BF16, align_bytes=64, name="x_grouped")
            grouped_words = grouped[:].bitcast(F32)
            for t2 in range(2):
                flip = psum.tile([P, PASSES * 2, P], F32, tag="bank")
                for g in range(PASSES):
                    for u in range(2):
                        nc.tensor.transpose(
                            flip[:, 2 * g + u, :], words[:, 2 * pair + t2, 2 * P * g + u : 2 * P * (g + 1) : 2], ident[:]
                        )
                nc.scalar.copy(
                    out=grouped_words[:, :, t2, :].rearrange("p g (i u) -> p g i u", u=2),
                    in_=flip[:].rearrange("p (g u) i -> p g i u", u=2),
                )
            return grouped

        def quantise_pair(grouped, x, pair):
            codes, scales = x
            nc.vector.quantize_mx(
                out=codes[:, pair].rearrange("p g c -> p (g c)").bitcast(FP8X4),
                scales=scales[:, pair].rearrange("p g c -> p (g c)"),
                in_=grouped[:].rearrange("p g t x -> p (g t x)"),
            )

        def add_passes(product, w, half, x, pair):
            w_codes, w_scales = w
            x_codes, x_scales = x
            features = slice(half * HD, (half + 1) * HD)
            for g in range(PASSES):
                nc.tensor.matmul_mx(
                    out=product[:, pair * 2 * P : (pair + 1) * 2 * P],
                    lhsT=w_codes[:, g, features].bitcast(FP8X4),
                    lhsT_scale=w_scales[:, g, features],
                    rhs=x_codes[:, pair, g, :].bitcast(FP8X4),
                    rhs_scale=x_scales[:, pair, g, :],
                    start=(g == 0),
                    stop=(g == PASSES - 1),
                )

        def project(w, half, x):
            product = psum.tile([P, WINDOWS], F32, tag="bank")
            for pair in range(TILES // 2):
                add_passes(product, w, half, x, pair)
            return product

        first_gate = soft.tile([P, 2, WINDOWS], F32)
        top_lo = soft.tile([P, WINDOWS], F32)
        top = soft.tile([P, WINDOWS], F32)
        x = []
        gate = {}

        def source(half):
            return slice(0, WINDOWS - 1) if half == LO else slice(0, WINDOWS)

        def window(half):
            return slice(1, WINDOWS) if half == LO else slice(0, WINDOWS)

        def multiply_gates(r):
            for half in (HI, LO):
                gate[(r, half)] = project(w_gate, half, x[r])

        def multiply_last_gates():
            r = RATIO - 1
            for half in (HI, LO):
                gate[(r, half)] = psum.tile([P, WINDOWS], F32, tag="bank", name="product")
            for pair in range(TILES // 2):
                for half in (HI, LO):
                    add_passes(gate[(r, half)], w_gate, half, x[r], pair)

        def split(half):
            first = window(half).start
            return [slice(first, WINDOWS // 2), slice(WINDOWS // 2, WINDOWS)]

        def shifted(half, part):
            return slice(part.start - 1, part.stop - 1) if half == LO else part

        def raise_top(r, half, out, before, cols):
            nc.vector.scalar_tensor_tensor(
                out=out, in0=gate[(r, half)][:, cols], scalar=offset(r, half), in1=before,
                op0=ALU.add, op1=ALU.max,
            )

        def largest_of_place(r, halves=(HI, LO)):
            if r == 0:
                for half in (HI, LO):
                    nc.scalar.activation(
                        out=first_gate[:, half, :], in_=gate[(r, half)][:], func=ACT.Identity, bias=offset(r, half)
                    )
            elif r == 1:
                for half, running in ((HI, top), (LO, top_lo)):
                    cols = source(half)
                    raise_top(r, half, running[:, cols], first_gate[:, half, cols], cols)
            else:
                for half in halves:
                    for part in split(half):
                        raise_top(r, half, top[:, part], top[:, part], shifted(half, part))

        def join_tops():
            for part in split(LO):
                nc.vector.tensor_tensor(
                    out=top[:, part], in0=top[:, part], in1=top_lo[:, shifted(LO, part)], op=ALU.max
                )

        wgate_grouped = regroup_weight(wgate_raw, nc.vector.tensor_copy)
        w_gate = quantise_weight(wgate_grouped)

        def take_in_pair(r, pair):
            if pair == 0:
                codes = tokens.tile([P, TILES // 2, PASSES, 2 * P], U32, align_bytes=64, name="x_codes")
                scales = tokens.tile([P, TILES // 2, PASSES, 2 * P], U8, align_bytes=64, name="x_scales")
                x.append((codes, scales))
            return transpose_pair(x_raw[r], pair)

        nc.vector.tensor_copy(out=ape_rows_f32[:], in_=ape_rows[:])
        for pair in range(TILES // 2):
            quantise_pair(take_in_pair(0, pair), x[0], pair)
        spread_ape()

        quantise_pair(take_in_pair(1, 0), x[1], 0)
        second = take_in_pair(1, 1)
        wkv_grouped = regroup_weight(wkv_raw, nc.vector.tensor_copy)
        quantise_pair(second, x[1], 1)
        multiply_gates(0)
        largest_of_place(0)
        w_kv = quantise_weight(wkv_grouped)

        quantise_pair(take_in_pair(2, 0), x[2], 0)
        second = take_in_pair(2, 1)
        multiply_gates(1)
        largest_of_place(1)
        quantise_pair(second, x[2], 1)
        join_tops()

        quantise_pair(take_in_pair(3, 0), x[3], 0)
        second = take_in_pair(3, 1)
        multiply_gates(2)
        largest_of_place(2, (HI,))
        quantise_pair(second, x[3], 1)
        largest_of_place(2, (LO,))
        multiply_last_gates()
        table_warmer = const.tile([P, 1], F32)
        nc.scalar.activation(out=table_warmer[:], in_=position[:, 0:1], func=ACT.Exp, scale=0.0)

        def lower(r, half, part=None):
            part = part or window(half)
            out = weight[:, half * RATIO + r, part]
            cols = shifted(half, part)
            if r == 0:
                nc.gpsimd.tensor_tensor(out=out, in0=first_gate[:, half, cols], in1=top[:, part], op=ALU.subtract)
            else:
                nc.vector.scalar_tensor_tensor(
                    out=out, in0=gate[(r, half)][:, cols], scalar=offset(r, half), in1=top[:, part],
                    op0=ALU.add, op1=ALU.subtract,
                )

        def exponential(r, half, part=None):
            one = weight[:, half * RATIO + r, part or window(half)]
            nc.scalar.activation(out=one, in_=one, func=ACT.Exp)

        kv = {}
        kv_copy = soft.tile([P, 2, WINDOWS], F32)

        def multiply_kv(r):
            for half in (LO, HI):
                kv[(r, half)] = project(w_kv, half, x[r])

        def weigh(r, halves=(LO, HI)):
            for half in halves:
                slot = half * RATIO + r
                out = weighted[:, slot, window(half)]
                one = weight[:, slot, window(half)]
                if r == 0:
                    nc.gpsimd.tensor_tensor(out=out, in0=one, in1=kv_copy[:, half, source(half)], op=ALU.mult)
                else:
                    nc.vector.tensor_tensor(out=out, in0=one, in1=kv[(r, half)][:, source(half)], op=ALU.mult)

        def add_up(total, terms, first, last):
            for t in range(TILES):
                nc.tensor.matmul(
                    out=total[:, t, :], lhsT=terms[:, t * P : (t + 1) * P], rhs=ident[:], is_transpose=True,
                    start=(first and t == 0), stop=(last and t == TILES - 1),
                )

        def add_all(total, terms, order, first=False, last=False):
            for n, (r, half) in enumerate(order):
                add_up(total, terms[:, half * RATIO + r, :], first and n == 0, last and n == len(order) - 1)

        multiply_kv(0)
        for half in (LO, HI):
            nc.scalar.copy(out=kv_copy[:, half, :], in_=kv[(0, half)][:])
        largest_of_place(RATIO - 1)
        for half in (HI, LO):
            lower(0, half)
        for part in split(LO):
            lower(1, LO, part)
            exponential(1, LO, part)
        lower(1, HI)
        exponential(1, HI)
        multiply_kv(1)
        lower(2, LO)
        lower(2, HI)
        exponential(0, HI)
        exponential(2, LO)
        exponential(2, HI)
        exponential(0, LO)
        weigh(0, (HI,))
        multiply_kv(2)
        lower(3, LO)
        lower(3, HI)
        exponential(3, LO)
        exponential(3, HI)
        nc.scalar.activation(
            out=table_warmer[:], in_=position[:, 0:1], func=ACT.Abs_reciprocal_sqrt, scale=0.0, bias=1.0
        )
        weigh(0, (LO,))
        multiply_kv(3)
        weight_sum = psum.tile([P, TILES, HD], F32, tag="bank")
        weighted_sum = psum.tile([P, TILES, HD], F32, tag="bank")
        for r in (1, 2, 3):
            weigh(r)
        for slot, (r, add) in enumerate(((2, nc.gpsimd.tensor_tensor), (3, nc.vector.tensor_tensor))):
            add(out=weighted_pair[:, slot, :], in0=weighted[:, r, :], in1=weighted[:, RATIO + r, :], op=ALU.add)
        add_all(weight_sum, weight, [(1, LO), (1, HI), (0, HI), (2, LO), (2, HI), (0, LO), (3, LO)], first=True)
        add_all(weighted_sum, weighted, [(1, LO)], first=True)
        add_all(weight_sum, weight, [(3, HI)], last=True)
        add_all(weighted_sum, weighted, [(1, HI), (0, HI), (0, LO)])
        for slot in (0, 1):
            add_up(weighted_sum, weighted_pair[:, slot, :], False, slot == 1)

        root = soft.tile([P, TILES, HD], F32)
        inverse = soft.tile([P, TILES, HD], F32)
        sides = [slice(0, TILES // 2), slice(TILES // 2, TILES)]
        for side in sides:
            nc.scalar.activation(out=root[:, side, :], in_=weight_sum[:, side, :], func=ACT.Abs_reciprocal_sqrt)
        for side in sides:
            nc.scalar.activation(out=inverse[:, side, :], in_=root[:, side, :], func=ACT.Square)

        shape = [P, TILES, HALF, 2]
        in_pairs = "p t (j e) -> p t j e"
        inverse_pairs = inverse[:, :, NOPE:HD].rearrange(in_pairs, e=2)
        sum_pairs = weighted_sum[:, :, NOPE:HD].rearrange(in_pairs, e=2)
        cos_inverse = soft.tile(shape, F32)
        nc.vector.tensor_tensor(
            out=cos_inverse[:], in0=inverse_pairs, in1=cos[:].unsqueeze(3).to_broadcast(shape), op=ALU.mult
        )
        sin_inverse = soft.tile(shape, F32)
        nc.vector.tensor_tensor(out=sin_inverse[:], in0=inverse_pairs, in1=cross_sin[:], op=ALU.mult)
        straight = soft.tile(shape, F32)
        nc.vector.tensor_tensor(out=straight[:], in0=sum_pairs, in1=cos_inverse[:], op=ALU.mult)
        crossed = soft.tile(shape, F32)
        nc.vector.tensor_tensor(out=crossed[:], in0=sum_pairs, in1=sin_inverse[:], op=ALU.mult)
        pooled = soft.tile([P, TILES, HD], F32)
        nc.vector.tensor_tensor(out=pooled[:], in0=weighted_sum[:], in1=inverse[:], op=ALU.mult)
        nc.sync.dma_start(out=pooled_rows, in_=pooled[:])
        k_rot = soft.tile([P, TILES, HD], F32)
        nc.scalar.copy(out=k_rot[:, :, 0:NOPE], in_=pooled[:, :, 0:NOPE])
        nc.vector.tensor_tensor(
            out=k_rot[:, :, NOPE:HD].rearrange(in_pairs, e=2), in0=straight[:], in1=crossed[:, :, :, ::-1], op=ALU.add
        )
        nc.sync.dma_start(out=k_rot_rows, in_=k_rot[:])
